import numpy as np
import ml_dtypes


def mxq(x, axis, fmt="e4m3"):
    dtype, down = {"e4m3": (ml_dtypes.float8_e4m3fn, 7), "e5m2": (ml_dtypes.float8_e5m2, 14)}[fmt]
    v = np.moveaxis(np.asarray(x, np.float32).astype(ml_dtypes.bfloat16).astype(np.float64), axis, -1)
    blocks = v.reshape(v.shape[:-1] + (-1, 32))
    amax = np.abs(blocks).max(-1, keepdims=True)
    byte = np.maximum(np.where(amax > 0, np.frexp(amax)[1] - 1 + 127, 0) - down, 1)
    scale = np.exp2(byte - 127.0)
    codes = (blocks / scale).astype(np.float32).astype(dtype).astype(np.float64)
    return np.moveaxis((codes * scale).reshape(v.shape), -1, axis)


WIDE = False


def mx_kscale(k):
    if not WIDE:
        return np.ones(k)
    levels = np.array([10, -10, 5, -5, 0])
    if k % 512:
        return np.exp2(np.random.permutation(np.resize(levels, k // 32))).repeat(32)
    a = np.empty((k // 512, 16))
    for p in range(k // 512):
        a[p, :8] = np.random.permutation(np.resize(levels, 8))
        for g in range(8):
            far = levels[np.abs(levels - a[p, g]) >= 10]
            a[p, g + 8] = far[np.random.randint(len(far))]
    return np.exp2(a.ravel()).repeat(32)


BF16 = ml_dtypes.bfloat16


def bf(x):
    return np.asarray(x, np.float32).astype(BF16)


def f64(x):
    return np.asarray(x).astype(np.float64)


B, N, D, F, C, L = 2048, 6144, 1024, 256, 128, 28
EPS = 1e-12


def l2norm(x):
    n = np.sqrt(np.sum(x * x, axis=1, keepdims=True))
    return x / np.maximum(n, EPS)


def setup_inputs():
    s = mx_kscale(D)
    return {"features": bf(np.random.standard_normal((B, D)) * s),
            "ex_features": bf(np.random.standard_normal((N, D)) * s),
            "g_weight": bf(np.random.standard_normal((F, D)) / np.sqrt(D) / s)}


def reference(features, ex_features, g_weight):
    gq = mxq(f64(g_weight), 1, "e4m3")
    f = mxq(f64(features), 1, "e4m3") @ gq.T
    exf = mxq(f64(ex_features), 1, "e4m3") @ gq.T
    return l2norm(f), l2norm(exf)

@@ -1,0 +1,219 @@
+import concourse.mybir as mybir
+from concourse.masks import make_identity
+
+F32 = mybir.dt.float32
+BF16 = mybir.dt.bfloat16
+U32 = mybir.dt.uint32
+U8 = mybir.dt.uint8
+FP8X4 = mybir.dt.float8_e4m3fn_x4
+ACT = mybir.ActivationFunctionType
+ALU = mybir.AluOpType
+
+P = 128
+PACK = 4
+K = 1024
+K_PASS = P * PACK
+PASSES = K // K_PASS
+PAIRS = PACK // 2
+BLOCKS = PASSES * PAIRS
+ROW_WORDS = K // 2
+F_OUT = 256
+F_TILES = F_OUT // P
+TILES = 4
+CHUNK_ROWS = P * TILES
+BANK_TILES = 2
+BANKS = TILES // BANK_TILES
+HALF_CODES = TILES * PASSES * P // 2
+LOADS_AHEAD = 7
+EPS = 1e-12
+
+FLOPS = 2 * (2048 + 6144) * K * F_OUT
+
+
+def transpose_rows(nc, flip_pool, identity, rows_words):
+    flipped = flip_pool.tile([P, BLOCKS, P], F32)
+    for b in range(BLOCKS):
+        g, u = divmod(b, PAIRS)
+        pass_words = slice(g * PAIRS * P + u, (g + 1) * PAIRS * P, PAIRS)
+        nc.tensor.transpose(flipped[:, b, :], rows_words[:, pass_words], identity[:])
+    return flipped
+
+
+def regroup(copy, flipped, grouped_words):
+    copy(out=grouped_words, in_=flipped[:].rearrange("p (g u) r -> p g r u", u=PAIRS))
+
+
+def tile_minerva_old_pa_t_kernel(tc, features, ex_features, g_weight, out_0, out_1):
+    nc = tc.nc
+
+    chunks = []
+    for src, dst in ((features, out_0), (ex_features, out_1)):
+        for row in range(0, src.shape[0], CHUNK_ROWS):
+            chunks.append((src[row : row + CHUNK_ROWS, :], dst[row : row + CHUNK_ROWS, :]))
+    n_chunks = len(chunks)
+
+    with tc.manual_schedule(), tc.tile_pool(name="keep", bufs=1) as keep, tc.tile_pool(
+        name="x", bufs=LOADS_AHEAD + 1
+    ) as x_pool, tc.tile_pool(name="operand", bufs=3) as operand_pool, tc.tile_pool(
+        name="small", bufs=4
+    ) as small_pool, tc.tile_pool(name="result", bufs=6) as result_pool, tc.psum_pool(
+        name="flip", bufs=TILES
+    ) as flip_pool, tc.psum_pool(name="product", bufs=2 * BANKS) as product_pool:
+        x_tiles = {}
+        flipped_tiles = {}
+        operands = {}
+        products = {}
+        sums = {}
+        results = {}
+
+        def load(c, pieces):
+            x_sb = x_pool.tile([P, TILES * K], BF16)
+            width = TILES * K // pieces
+            rows = chunks[c][0].rearrange("(p t) k -> p (t k)", t=TILES)
+            for piece in range(pieces):
+                cols = slice(piece * width, (piece + 1) * width)
+                nc.sync.dma_start(out=x_sb[:, cols], in_=rows[:, cols])
+            x_tiles[c] = x_sb
+
+        def transpose(c):
+            words = x_tiles[c][:].bitcast(F32)
+            flipped_tiles[c] = [
+                transpose_rows(nc, flip_pool, identity, words[:, t * ROW_WORDS : (t + 1) * ROW_WORDS])
+                for t in range(TILES)
+            ]
+            grouped = operand_pool.tile([P, TILES * K], BF16, align_bytes=64)
+            codes = operand_pool.tile([P, 2 * HALF_CODES], U32, align_bytes=64)
+            scales = operand_pool.tile([P, 2 * HALF_CODES], U8, align_bytes=64)
+            operands[c] = (grouped, codes, scales)
+
+        def regroup_tile(copy, c, t):
+            grouped_words = operands[c][0][:].bitcast(F32).rearrange(
+                "p (t g r u) -> p t g r u", t=TILES, g=PASSES, u=PAIRS
+            )
+            regroup(copy, flipped_tiles[c][t], grouped_words[:, t])
+
+        def quantise(c, half):
+            grouped, codes, scales = operands[c]
+            cols = slice(half * HALF_CODES, (half + 1) * HALF_CODES)
+            nc.vector.quantize_mx(
+                out=codes[:, cols].bitcast(FP8X4),
+                scales=scales[:, cols],
+                in_=grouped[:, half * HALF_CODES * PACK : (half + 1) * HALF_CODES * PACK],
+            )
+
+        def multiply(c):
+            grouped, codes, scales = operands[c]
+            products[c] = []
+            for h in range(BANKS):
+                product = product_pool.tile([P, BANK_TILES, F_OUT], F32)
+                products[c].append(product)
+                for s in range(BANK_TILES):
+                    for g in range(PASSES):
+                        first = ((h * BANK_TILES + s) * PASSES + g) * P
+                        row_cols = slice(first, first + P)
+                        outs = slice(g * F_OUT, (g + 1) * F_OUT)
+                        nc.tensor.matmul_mx(
+                            out=product[:, s, :],
+                            lhsT=codes[:, row_cols].bitcast(FP8X4),
+                            lhsT_scale=scales[:, row_cols],
+                            rhs=w_codes[:, outs].bitcast(FP8X4),
+                            rhs_scale=w_scales[:, outs],
+                            start=(g == 0),
+                            stop=(g == PASSES - 1),
+                        )
+
+        def square_and_sum(c):
+            sum_sq = small_pool.tile([P, TILES], F32)
+            for t in range(TILES):
+                unread = small_pool.tile([P, F_OUT], F32)
+                nc.scalar.activation(
+                    out=unread[:],
+                    in_=products[c][t // BANK_TILES][:, t % BANK_TILES, :],
+                    func=ACT.Square,
+                    accum_out=sum_sq[:, t : t + 1],
+                )
+            sums[c] = sum_sq
+
+        def inverse_norms(c):
+            inverse = small_pool.tile([P, TILES], F32)
+            nc.scalar.activation(out=inverse[:], in_=sums[c][:], func=ACT.Abs_reciprocal_sqrt)
+            sums[c] = inverse
+            result = result_pool.tile([P, TILES * F_OUT], F32)
+            results[c] = result
+
+        def scale(c, h):
+            tiles = slice(h * BANK_TILES, (h + 1) * BANK_TILES)
+            nc.vector.scalar_tensor_tensor(
+                out=results[c][:].rearrange("p (t f) -> p t f", t=TILES)[:, tiles, :],
+                in0=sums[c][:, tiles].unsqueeze(2).to_broadcast([P, BANK_TILES, F_OUT]),
+                scalar=1.0 / EPS,
+                in1=products[c][h][:],
+                op0=ALU.min,
+                op1=ALU.mult,
+            )
+
+        def store(c):
+            nc.sync.dma_start(
+                out=chunks[c][1].rearrange("(p t) f -> p (t f)", t=TILES), in_=results[c][:]
+            )
+
+        w_sb = keep.tile([P, F_TILES * K], BF16)
+        nc.sync.dma_start(
+            out=w_sb[:].rearrange("p (j k) -> p j k", j=F_TILES),
+            in_=g_weight.rearrange("(j p) k -> p j k", p=P),
+        )
+        load(0, TILES)
+        for c in range(1, LOADS_AHEAD):
+            load(c, 1)
+
+        identity = keep.tile([P, P], F32)
+        make_identity(nc, identity[:])
+
+        one = keep.tile([P, 1], F32)
+        nc.vector.memset(one[:], 1.0)
+        warm = keep.tile([P, 1], F32)
+        nc.scalar.activation(out=warm[:], in_=one[:], func=ACT.Abs_reciprocal_sqrt)
+
+        w_grouped = keep.tile([P, PASSES * F_OUT * PACK], BF16, align_bytes=64)
+        w_codes = keep.tile([P, PASSES * F_OUT], U32, align_bytes=64)
+        w_scales = keep.tile([P, PASSES * F_OUT], U8, align_bytes=64)
+        w_words = w_sb[:].bitcast(F32)
+        w_grouped_words = w_grouped[:].bitcast(F32).rearrange(
+            "p (g j r u) -> p j g r u", g=PASSES, j=F_TILES, u=PAIRS
+        )
+        w_copies = (nc.vector.tensor_copy, nc.scalar.copy)
+        for j in range(F_TILES):
+            w_flipped = transpose_rows(
+                nc, flip_pool, identity, w_words[:, j * ROW_WORDS : (j + 1) * ROW_WORDS]
+            )
+            regroup(w_copies[j], w_flipped, w_grouped_words[:, j])
+        nc.vector.quantize_mx(out=w_codes[:].bitcast(FP8X4), scales=w_scales[:], in_=w_grouped[:])
+
+        for i in range(n_chunks + 2):
+            fresh = i < n_chunks
+            multiplied = 1 <= i <= n_chunks
+            summed = i >= 2
+            if i + LOADS_AHEAD < n_chunks:
+                load(i + LOADS_AHEAD, 1)
+            if fresh:
+                transpose(i)
+            if multiplied:
+                multiply(i - 1)
+            if fresh:
+                regroup_tile(nc.scalar.copy, i, 0)
+                regroup_tile(nc.scalar.copy, i, 1)
+            if summed:
+                inverse_norms(i - 2)
+            if fresh:
+                regroup_tile(nc.scalar.copy, i, 2)
+                regroup_tile(nc.vector.tensor_copy, i, 3)
+                quantise(i, 0)
+            if summed:
+                scale(i - 2, 0)
+            if fresh:
+                quantise(i, 1)
+            if summed:
+                scale(i - 2, 1)
+                store(i - 2)
+            if multiplied:
+                square_and_sum(i - 1)

@@ -21,9 +21,9 @@ F_OUT = 256
 F_TILES = F_OUT // P
 TILES = 4
 CHUNK_ROWS = P * TILES
-BANK_TILES = 2
-BANKS = TILES // BANK_TILES
-HALF_CODES = TILES * PASSES * P // 2
+GROUP_TILES = 2
+GROUPS = TILES // GROUP_TILES
+GROUP_CODES = GROUP_TILES * PASSES * P
 LOADS_AHEAD = 7
 EPS = 1e-12
 
@@ -51,19 +51,21 @@ def tile_minerva_old_pa_t_kernel(tc, features, ex_features, g_weight, out_0, out
         for row in range(0, src.shape[0], CHUNK_ROWS):
             chunks.append((src[row : row + CHUNK_ROWS, :], dst[row : row + CHUNK_ROWS, :]))
     n_chunks = len(chunks)
+    n_groups = n_chunks * GROUPS
 
     with tc.manual_schedule(), tc.tile_pool(name="keep", bufs=1) as keep, tc.tile_pool(
         name="x", bufs=LOADS_AHEAD + 1
-    ) as x_pool, tc.tile_pool(name="operand", bufs=3) as operand_pool, tc.tile_pool(
+    ) as x_pool, tc.tile_pool(name="operand", bufs=4) as operand_pool, tc.tile_pool(
         name="small", bufs=4
     ) as small_pool, tc.tile_pool(name="result", bufs=6) as result_pool, tc.psum_pool(
-        name="flip", bufs=TILES
-    ) as flip_pool, tc.psum_pool(name="product", bufs=2 * BANKS) as product_pool:
+        name="flip", bufs=2 * GROUP_TILES
+    ) as flip_pool, tc.psum_pool(name="product", bufs=4) as product_pool:
         x_tiles = {}
         flipped_tiles = {}
         operands = {}
         products = {}
         sums = {}
+        inverses = {}
         results = {}
 
         def load(c, pieces):
@@ -75,86 +77,86 @@ def tile_minerva_old_pa_t_kernel(tc, features, ex_features, g_weight, out_0, out
                 nc.sync.dma_start(out=x_sb[:, cols], in_=rows[:, cols])
             x_tiles[c] = x_sb
 
-        def transpose(c):
+        def transpose(h):
+            c, half = divmod(h, GROUPS)
             words = x_tiles[c][:].bitcast(F32)
-            flipped_tiles[c] = [
-                transpose_rows(nc, flip_pool, identity, words[:, t * ROW_WORDS : (t + 1) * ROW_WORDS])
-                for t in range(TILES)
-            ]
-            grouped = operand_pool.tile([P, TILES * K], BF16, align_bytes=64)
-            codes = operand_pool.tile([P, 2 * HALF_CODES], U32, align_bytes=64)
-            scales = operand_pool.tile([P, 2 * HALF_CODES], U8, align_bytes=64)
-            operands[c] = (grouped, codes, scales)
+            flipped_tiles[h] = []
+            for s in range(GROUP_TILES):
+                first = (half * GROUP_TILES + s) * ROW_WORDS
+                flipped_tiles[h].append(
+                    transpose_rows(nc, flip_pool, identity, words[:, first : first + ROW_WORDS])
+                )
+            grouped = operand_pool.tile([P, GROUP_CODES * PACK], BF16, align_bytes=64)
+            codes = operand_pool.tile([P, GROUP_CODES], U32, align_bytes=64)
+            scales = operand_pool.tile([P, GROUP_CODES], U8, align_bytes=64)
+            operands[h] = (grouped, codes, scales)
 
-        def regroup_tile(copy, c, t):
-            grouped_words = operands[c][0][:].bitcast(F32).rearrange(
-                "p (t g r u) -> p t g r u", t=TILES, g=PASSES, u=PAIRS
+        def regroup_tile(copy, h, s):
+            grouped_words = operands[h][0][:].bitcast(F32).rearrange(
+                "p (s g r u) -> p s g r u", s=GROUP_TILES, g=PASSES, u=PAIRS
             )
-            regroup(copy, flipped_tiles[c][t], grouped_words[:, t])
+            regroup(copy, flipped_tiles[h][s], grouped_words[:, s])
 
-        def quantise(c, half):
-            grouped, codes, scales = operands[c]
-            cols = slice(half * HALF_CODES, (half + 1) * HALF_CODES)
-            nc.vector.quantize_mx(
-                out=codes[:, cols].bitcast(FP8X4),
-                scales=scales[:, cols],
-                in_=grouped[:, half * HALF_CODES * PACK : (half + 1) * HALF_CODES * PACK],
-            )
+        def quantise(h):
+            grouped, codes, scales = operands[h]
+            nc.vector.quantize_mx(out=codes[:].bitcast(FP8X4), scales=scales[:], in_=grouped[:])
 
-        def multiply(c):
-            grouped, codes, scales = operands[c]
-            products[c] = []
-            for h in range(BANKS):
-                product = product_pool.tile([P, BANK_TILES, F_OUT], F32)
-                products[c].append(product)
-                for s in range(BANK_TILES):
-                    for g in range(PASSES):
-                        first = ((h * BANK_TILES + s) * PASSES + g) * P
-                        row_cols = slice(first, first + P)
-                        outs = slice(g * F_OUT, (g + 1) * F_OUT)
-                        nc.tensor.matmul_mx(
-                            out=product[:, s, :],
-                            lhsT=codes[:, row_cols].bitcast(FP8X4),
-                            lhsT_scale=scales[:, row_cols],
-                            rhs=w_codes[:, outs].bitcast(FP8X4),
-                            rhs_scale=w_scales[:, outs],
-                            start=(g == 0),
-                            stop=(g == PASSES - 1),
-                        )
+        def multiply(h):
+            grouped, codes, scales = operands[h]
+            product = product_pool.tile([P, GROUP_TILES, F_OUT], F32)
+            products[h] = product
+            for s in range(GROUP_TILES):
+                for g in range(PASSES):
+                    first = (s * PASSES + g) * P
+                    row_cols = slice(first, first + P)
+                    outs = slice(g * F_OUT, (g + 1) * F_OUT)
+                    nc.tensor.matmul_mx(
+                        out=product[:, s, :],
+                        lhsT=codes[:, row_cols].bitcast(FP8X4),
+                        lhsT_scale=scales[:, row_cols],
+                        rhs=w_codes[:, outs].bitcast(FP8X4),
+                        rhs_scale=w_scales[:, outs],
+                        start=(g == 0),
+                        stop=(g == PASSES - 1),
+                    )
 
-        def square_and_sum(c):
-            sum_sq = small_pool.tile([P, TILES], F32)
-            for t in range(TILES):
+        def square_and_sum(h):
+            sum_sq = small_pool.tile([P, GROUP_TILES], F32)
+            for s in range(GROUP_TILES):
                 unread = small_pool.tile([P, F_OUT], F32)
                 nc.scalar.activation(
                     out=unread[:],
-                    in_=products[c][t // BANK_TILES][:, t % BANK_TILES, :],
+                    in_=products[h][:, s, :],
                     func=ACT.Square,
-                    accum_out=sum_sq[:, t : t + 1],
+                    accum_out=sum_sq[:, s : s + 1],
                 )
-            sums[c] = sum_sq
+            sums[h] = sum_sq
 
-        def inverse_norms(c):
-            inverse = small_pool.tile([P, TILES], F32)
-            nc.scalar.activation(out=inverse[:], in_=sums[c][:], func=ACT.Abs_reciprocal_sqrt)
-            sums[c] = inverse
-            result = result_pool.tile([P, TILES * F_OUT], F32)
-            results[c] = result
+        def inverse_norms(h):
+            inverse = small_pool.tile([P, GROUP_TILES], F32)
+            nc.scalar.activation(out=inverse[:], in_=sums[h][:], func=ACT.Abs_reciprocal_sqrt)
+            inverses[h] = inverse
 
-        def scale(c, h):
-            tiles = slice(h * BANK_TILES, (h + 1) * BANK_TILES)
+        def scale(h):
+            c, half = divmod(h, GROUPS)
+            if half == 0:
+                result = result_pool.tile([P, TILES, F_OUT], F32)
+                results[c] = result
             nc.vector.scalar_tensor_tensor(
-                out=results[c][:].rearrange("p (t f) -> p t f", t=TILES)[:, tiles, :],
-                in0=sums[c][:, tiles].unsqueeze(2).to_broadcast([P, BANK_TILES, F_OUT]),
+                out=results[c][:, half * GROUP_TILES : (half + 1) * GROUP_TILES, :],
+                in0=inverses[h][:].unsqueeze(2).to_broadcast([P, GROUP_TILES, F_OUT]),
                 scalar=1.0 / EPS,
-                in1=products[c][h][:],
+                in1=products[h][:],
                 op0=ALU.min,
                 op1=ALU.mult,
             )
 
-        def store(c):
+        def store(c, first_tile, tiles):
             nc.sync.dma_start(
-                out=chunks[c][1].rearrange("(p t) f -> p (t f)", t=TILES), in_=results[c][:]
+                out=chunks[c][1].rearrange("(p t) f -> p t f", t=TILES)[
+                    :, first_tile : first_tile + tiles, :
+                ],
+                in_=results[c][:, first_tile : first_tile + tiles, :],
             )
 
         w_sb = keep.tile([P, F_TILES * K], BF16)
@@ -189,31 +191,28 @@ def tile_minerva_old_pa_t_kernel(tc, features, ex_features, g_weight, out_0, out
             regroup(w_copies[j], w_flipped, w_grouped_words[:, j])
         nc.vector.quantize_mx(out=w_codes[:].bitcast(FP8X4), scales=w_scales[:], in_=w_grouped[:])
 
-        for i in range(n_chunks + 2):
-            fresh = i < n_chunks
-            multiplied = 1 <= i <= n_chunks
-            summed = i >= 2
-            if i + LOADS_AHEAD < n_chunks:
-                load(i + LOADS_AHEAD, 1)
-            if fresh:
+        for i in range(n_groups + 4):
+            c, half = divmod(i, GROUPS)
+            if half == 0 and c + LOADS_AHEAD < n_chunks:
+                load(c + LOADS_AHEAD, 1)
+            if i < n_groups:
                 transpose(i)
-            if multiplied:
-                multiply(i - 1)
-            if fresh:
+            if 1 <= i <= n_groups:
+                quantise(i - 1)
+            if 2 <= i <= n_groups + 1:
+                multiply(i - 2)
+            if 3 <= i <= n_groups + 2:
+                square_and_sum(i - 3)
+            if i >= 4:
+                scale(i - 4)
+            if i < n_groups:
                 regroup_tile(nc.scalar.copy, i, 0)
-                regroup_tile(nc.scalar.copy, i, 1)
-            if summed:
-                inverse_norms(i - 2)
-            if fresh:
-                regroup_tile(nc.scalar.copy, i, 2)
-                regroup_tile(nc.vector.tensor_copy, i, 3)
-                quantise(i, 0)
-            if summed:
-                scale(i - 2, 0)
-            if fresh:
-                quantise(i, 1)
-            if summed:
-                scale(i - 2, 1)
-                store(i - 2)
-            if multiplied:
-                square_and_sum(i - 1)
+                regroup_tile(nc.scalar.copy if half == 0 else nc.vector.tensor_copy, i, 1)
+            if 3 <= i <= n_groups + 2:
+                inverse_norms(i - 3)
+            if i >= 4:
+                c, half = divmod(i - 4, GROUPS)
+                if c == n_chunks - 1:
+                    store(c, half * GROUP_TILES, GROUP_TILES)
+                elif half == GROUPS - 1:
+                    store(c, 0, TILES)

@@ -23,7 +23,9 @@ TILES = 4
 CHUNK_ROWS = P * TILES
 GROUP_TILES = 2
 GROUPS = TILES // GROUP_TILES
-GROUP_CODES = GROUP_TILES * PASSES * P
+TILE_CODES = PASSES * P
+GROUP_CODES = GROUP_TILES * TILE_CODES
+FINE_CHUNKS = 3
 LOADS_AHEAD = 7
 EPS = 1e-12
 
@@ -68,14 +70,30 @@ def tile_minerva_old_pa_t_kernel(tc, features, ex_features, g_weight, out_0, out
         inverses = {}
         results = {}
 
-        def load(c, pieces):
-            x_sb = x_pool.tile([P, TILES * K], BF16)
-            width = TILES * K // pieces
+        def load(c, first_tile, tiles):
+            if first_tile == 0:
+                x_sb = x_pool.tile([P, TILES * K], BF16)
+                x_tiles[c] = x_sb
             rows = chunks[c][0].rearrange("(p t) k -> p (t k)", t=TILES)
-            for piece in range(pieces):
-                cols = slice(piece * width, (piece + 1) * width)
-                nc.sync.dma_start(out=x_sb[:, cols], in_=rows[:, cols])
-            x_tiles[c] = x_sb
+            cols = slice(first_tile * K, (first_tile + tiles) * K)
+            nc.sync.dma_start(out=x_tiles[c][:, cols], in_=rows[:, cols])
+
+        def transpose_weight():
+            w_words = w_sb[:].bitcast(F32)
+            w_grouped_words = w_grouped[:].bitcast(F32).rearrange(
+                "p (g j r u) -> p j g r u", g=PASSES, j=F_TILES, u=PAIRS
+            )
+            w_copies = (nc.vector.tensor_copy, nc.scalar.copy)
+            for j in range(F_TILES):
+                w_flipped = transpose_rows(
+                    nc, flip_pool, identity, w_words[:, j * ROW_WORDS : (j + 1) * ROW_WORDS]
+                )
+                regroup(w_copies[j], w_flipped, w_grouped_words[:, j])
+
+        def quantise_weight():
+            nc.vector.quantize_mx(
+                out=w_codes[:].bitcast(FP8X4), scales=w_scales[:], in_=w_grouped[:]
+            )
 
         def transpose(h):
             c, half = divmod(h, GROUPS)
@@ -97,21 +115,26 @@ def tile_minerva_old_pa_t_kernel(tc, features, ex_features, g_weight, out_0, out
             )
             regroup(copy, flipped_tiles[h][s], grouped_words[:, s])
 
-        def quantise(h):
+        def quantise(h, first_tile=0, tiles=GROUP_TILES):
             grouped, codes, scales = operands[h]
-            nc.vector.quantize_mx(out=codes[:].bitcast(FP8X4), scales=scales[:], in_=grouped[:])
+            cols = slice(first_tile * TILE_CODES, (first_tile + tiles) * TILE_CODES)
+            values = slice(cols.start * PACK, cols.stop * PACK)
+            nc.vector.quantize_mx(
+                out=codes[:, cols].bitcast(FP8X4), scales=scales[:, cols], in_=grouped[:, values]
+            )
 
-        def multiply(h):
+        def multiply(h, first_tile=0, tiles=GROUP_TILES):
             grouped, codes, scales = operands[h]
-            product = product_pool.tile([P, GROUP_TILES, F_OUT], F32)
-            products[h] = product
-            for s in range(GROUP_TILES):
+            if first_tile == 0:
+                product = product_pool.tile([P, GROUP_TILES, F_OUT], F32)
+                products[h] = product
+            for s in range(first_tile, first_tile + tiles):
                 for g in range(PASSES):
                     first = (s * PASSES + g) * P
                     row_cols = slice(first, first + P)
                     outs = slice(g * F_OUT, (g + 1) * F_OUT)
                     nc.tensor.matmul_mx(
-                        out=product[:, s, :],
+                        out=products[h][:, s, :],
                         lhsT=codes[:, row_cols].bitcast(FP8X4),
                         lhsT_scale=scales[:, row_cols],
                         rhs=w_codes[:, outs].bitcast(FP8X4),
@@ -120,33 +143,36 @@ def tile_minerva_old_pa_t_kernel(tc, features, ex_features, g_weight, out_0, out
                         stop=(g == PASSES - 1),
                     )
 
-        def square_and_sum(h):
-            sum_sq = small_pool.tile([P, GROUP_TILES], F32)
-            for s in range(GROUP_TILES):
+        def square_and_sum(h, first_tile=0, tiles=GROUP_TILES):
+            sum_sq = small_pool.tile([P, tiles], F32)
+            for s in range(tiles):
                 unread = small_pool.tile([P, F_OUT], F32)
                 nc.scalar.activation(
                     out=unread[:],
-                    in_=products[h][:, s, :],
+                    in_=products[h][:, first_tile + s, :],
                     func=ACT.Square,
                     accum_out=sum_sq[:, s : s + 1],
                 )
-            sums[h] = sum_sq
+            sums[h, first_tile] = sum_sq
 
-        def inverse_norms(h):
-            inverse = small_pool.tile([P, GROUP_TILES], F32)
-            nc.scalar.activation(out=inverse[:], in_=sums[h][:], func=ACT.Abs_reciprocal_sqrt)
-            inverses[h] = inverse
+        def inverse_norms(h, first_tile=0, tiles=GROUP_TILES):
+            inverse = small_pool.tile([P, tiles], F32)
+            nc.scalar.activation(
+                out=inverse[:], in_=sums[h, first_tile][:], func=ACT.Abs_reciprocal_sqrt
+            )
+            inverses[h, first_tile] = inverse
 
-        def scale(h):
+        def scale(h, first_tile=0, tiles=GROUP_TILES):
             c, half = divmod(h, GROUPS)
-            if half == 0:
+            if half == 0 and first_tile == 0:
                 result = result_pool.tile([P, TILES, F_OUT], F32)
                 results[c] = result
+            t = half * GROUP_TILES + first_tile
             nc.vector.scalar_tensor_tensor(
-                out=results[c][:, half * GROUP_TILES : (half + 1) * GROUP_TILES, :],
-                in0=inverses[h][:].unsqueeze(2).to_broadcast([P, GROUP_TILES, F_OUT]),
+                out=results[c][:, t : t + tiles, :],
+                in0=inverses[h, first_tile][:].unsqueeze(2).to_broadcast([P, tiles, F_OUT]),
                 scalar=1.0 / EPS,
-                in1=products[h][:],
+                in1=products[h][:, first_tile : first_tile + tiles, :],
                 op0=ALU.min,
                 op1=ALU.mult,
             )
@@ -159,15 +185,30 @@ def tile_minerva_old_pa_t_kernel(tc, features, ex_features, g_weight, out_0, out
                 in_=results[c][:, first_tile : first_tile + tiles, :],
             )
 
+        def store_group(h):
+            c, half = divmod(h, GROUPS)
+            if c >= n_chunks - FINE_CHUNKS:
+                store(c, half * GROUP_TILES, GROUP_TILES)
+            elif half == GROUPS - 1:
+                store(c, 0, TILES)
+
         w_sb = keep.tile([P, F_TILES * K], BF16)
+        load(0, 0, 1)
+        load(0, 1, 1)
         nc.sync.dma_start(
             out=w_sb[:].rearrange("p (j k) -> p j k", j=F_TILES),
             in_=g_weight.rearrange("(j p) k -> p j k", p=P),
         )
-        load(0, TILES)
-        for c in range(1, LOADS_AHEAD):
-            load(c, 1)
+        load(0, 2, 1)
+        load(0, 3, 1)
+        for half in range(GROUPS):
+            load(1, half * GROUP_TILES, GROUP_TILES)
+        for c in range(2, LOADS_AHEAD):
+            load(c, 0, TILES)
 
+        w_grouped = keep.tile([P, PASSES * F_OUT * PACK], BF16, align_bytes=64)
+        w_codes = keep.tile([P, PASSES * F_OUT], U32, align_bytes=64)
+        w_scales = keep.tile([P, PASSES * F_OUT], U8, align_bytes=64)
         identity = keep.tile([P, P], F32)
         make_identity(nc, identity[:])
 
@@ -176,43 +217,52 @@ def tile_minerva_old_pa_t_kernel(tc, features, ex_features, g_weight, out_0, out
         warm = keep.tile([P, 1], F32)
         nc.scalar.activation(out=warm[:], in_=one[:], func=ACT.Abs_reciprocal_sqrt)
 
-        w_grouped = keep.tile([P, PASSES * F_OUT * PACK], BF16, align_bytes=64)
-        w_codes = keep.tile([P, PASSES * F_OUT], U32, align_bytes=64)
-        w_scales = keep.tile([P, PASSES * F_OUT], U8, align_bytes=64)
-        w_words = w_sb[:].bitcast(F32)
-        w_grouped_words = w_grouped[:].bitcast(F32).rearrange(
-            "p (g j r u) -> p j g r u", g=PASSES, j=F_TILES, u=PAIRS
-        )
-        w_copies = (nc.vector.tensor_copy, nc.scalar.copy)
-        for j in range(F_TILES):
-            w_flipped = transpose_rows(
-                nc, flip_pool, identity, w_words[:, j * ROW_WORDS : (j + 1) * ROW_WORDS]
-            )
-            regroup(w_copies[j], w_flipped, w_grouped_words[:, j])
-        nc.vector.quantize_mx(out=w_codes[:].bitcast(FP8X4), scales=w_scales[:], in_=w_grouped[:])
-
-        for i in range(n_groups + 4):
+        last = n_groups - 1
+        for i in range(n_groups):
             c, half = divmod(i, GROUPS)
             if half == 0 and c + LOADS_AHEAD < n_chunks:
-                load(c + LOADS_AHEAD, 1)
-            if i < n_groups:
-                transpose(i)
-            if 1 <= i <= n_groups:
+                load(c + LOADS_AHEAD, 0, TILES)
+            transpose(i)
+            if i >= 1:
                 quantise(i - 1)
-            if 2 <= i <= n_groups + 1:
+            if i == 3:
+                multiply(0)
+            if i >= 3:
                 multiply(i - 2)
-            if 3 <= i <= n_groups + 2:
+            if i >= 3:
                 square_and_sum(i - 3)
             if i >= 4:
                 scale(i - 4)
-            if i < n_groups:
-                regroup_tile(nc.scalar.copy, i, 0)
-                regroup_tile(nc.scalar.copy if half == 0 else nc.vector.tensor_copy, i, 1)
-            if 3 <= i <= n_groups + 2:
+            regroup_tile(nc.scalar.copy, i, 0)
+            regroup_tile(nc.scalar.copy if half == 0 else nc.vector.tensor_copy, i, 1)
+            if i == 0:
+                transpose_weight()
+            if i == 1:
+                quantise_weight()
+            if i >= 3:
                 inverse_norms(i - 3)
             if i >= 4:
-                c, half = divmod(i - 4, GROUPS)
-                if c == n_chunks - 1:
-                    store(c, half * GROUP_TILES, GROUP_TILES)
-                elif half == GROUPS - 1:
-                    store(c, 0, TILES)
+                store_group(i - 4)
+
+        for s in range(GROUP_TILES):
+            quantise(last, s, 1)
+        multiply(last - 1)
+        for s in range(GROUP_TILES):
+            multiply(last, s, 1)
+        scale(last - 3)
+        store_group(last - 3)
+        square_and_sum(last - 2)
+        square_and_sum(last - 1)
+        inverse_norms(last - 2)
+        scale(last - 2)
+        store_group(last - 2)
+        inverse_norms(last - 1)
+        scale(last - 1)
+        store_group(last - 1)
+        for s in range(GROUP_TILES):
+            square_and_sum(last, s, 1)
+        for s in range(GROUP_TILES):
+            inverse_norms(last, s, 1)
+        for s in range(GROUP_TILES):
+            scale(last, s, 1)
+            store(n_chunks - 1, GROUP_TILES + s, 1)

@@ -32,13 +32,23 @@ EPS = 1e-12
 FLOPS = 2 * (2048 + 6144) * K * F_OUT
 
 
-def transpose_rows(nc, flip_pool, identity, rows_words):
+def transpose_rows(nc, flip_pool, identity, rows_words, in_order=False):
     flipped = flip_pool.tile([P, BLOCKS, P], F32)
     for b in range(BLOCKS):
         g, u = divmod(b, PAIRS)
-        pass_words = slice(g * PAIRS * P + u, (g + 1) * PAIRS * P, PAIRS)
-        nc.tensor.transpose(flipped[:, b, :], rows_words[:, pass_words], identity[:])
+        if in_order:
+            block_words = slice(b * P, (b + 1) * P)
+        else:
+            block_words = slice(g * PAIRS * P + u, (g + 1) * PAIRS * P, PAIRS)
+        nc.tensor.transpose(flipped[:, b, :], rows_words[:, block_words], identity[:])
     return flipped
+
+
+def sort_words(copy, ordered_words, rows_words):
+    copy(
+        out=ordered_words.rearrange("r (g u j) -> r g u j", g=PASSES, u=PAIRS),
+        in_=rows_words.rearrange("r (g j u) -> r g u j", g=PASSES, u=PAIRS),
+    )
 
 
 def regroup(copy, flipped, grouped_words):
@@ -57,12 +67,15 @@ def tile_minerva_old_pa_t_kernel(tc, features, ex_features, g_weight, out_0, out
 
     with tc.manual_schedule(), tc.tile_pool(name="keep", bufs=1) as keep, tc.tile_pool(
         name="x", bufs=LOADS_AHEAD + 1
-    ) as x_pool, tc.tile_pool(name="operand", bufs=4) as operand_pool, tc.tile_pool(
+    ) as x_pool, tc.tile_pool(name="ordered", bufs=2) as ordered_pool, tc.tile_pool(
+        name="operand", bufs=4
+    ) as operand_pool, tc.tile_pool(
         name="small", bufs=4
     ) as small_pool, tc.tile_pool(name="result", bufs=6) as result_pool, tc.psum_pool(
         name="flip", bufs=2 * GROUP_TILES
     ) as flip_pool, tc.psum_pool(name="product", bufs=4) as product_pool:
         x_tiles = {}
+        ordered_tiles = {}
         flipped_tiles = {}
         operands = {}
         products = {}
@@ -95,15 +108,26 @@ def tile_minerva_old_pa_t_kernel(tc, features, ex_features, g_weight, out_0, out
                 out=w_codes[:].bitcast(FP8X4), scales=w_scales[:], in_=w_grouped[:]
             )
 
-        def transpose(h):
+        def tile_words(h, s):
             c, half = divmod(h, GROUPS)
-            words = x_tiles[c][:].bitcast(F32)
+            first = (half * GROUP_TILES + s) * ROW_WORDS
+            return x_tiles[c][:].bitcast(F32)[:, first : first + ROW_WORDS]
+
+        def sort(h, s):
+            ordered = ordered_pool.tile([P, ROW_WORDS], F32)
+            sort_words(nc.gpsimd.tensor_copy, ordered[:], tile_words(h, s))
+            ordered_tiles[h, s] = ordered
+
+        def follow(h):
+            word = ordered_pool.tile([P, 1], U32)
+            nc.gpsimd.tensor_copy(out=word[:], in_=operands[h][1][:, 0:1])
+
+        def transpose(h):
             flipped_tiles[h] = []
             for s in range(GROUP_TILES):
-                first = (half * GROUP_TILES + s) * ROW_WORDS
-                flipped_tiles[h].append(
-                    transpose_rows(nc, flip_pool, identity, words[:, first : first + ROW_WORDS])
-                )
+                in_order = (h, s) in ordered_tiles
+                words = ordered_tiles[h, s][:] if in_order else tile_words(h, s)
+                flipped_tiles[h].append(transpose_rows(nc, flip_pool, identity, words, in_order))
             grouped = operand_pool.tile([P, GROUP_CODES * PACK], BF16, align_bytes=64)
             codes = operand_pool.tile([P, GROUP_CODES], U32, align_bytes=64)
             scales = operand_pool.tile([P, GROUP_CODES], U8, align_bytes=64)
@@ -225,24 +249,26 @@ def tile_minerva_old_pa_t_kernel(tc, features, ex_features, g_weight, out_0, out
             transpose(i)
             if i >= 1:
                 quantise(i - 1)
+            if half == 0 and 1 <= i < n_groups - GROUPS:
+                follow(i - 1)
+                sort(i + GROUPS, GROUP_TILES - 1)
             if i == 3:
                 multiply(0)
             if i >= 3:
                 multiply(i - 2)
             if i >= 3:
                 square_and_sum(i - 3)
-            if i >= 4:
-                scale(i - 4)
             regroup_tile(nc.scalar.copy, i, 0)
-            regroup_tile(nc.scalar.copy if half == 0 else nc.vector.tensor_copy, i, 1)
+            regroup_tile(nc.vector.tensor_copy if half == 0 else nc.scalar.copy, i, 1)
             if i == 0:
                 transpose_weight()
             if i == 1:
                 quantise_weight()
+            if i >= 4:
+                scale(i - 4)
+                store_group(i - 4)
             if i >= 3:
                 inverse_norms(i - 3)
-            if i >= 4:
-                store_group(i - 4)
 
         for s in range(GROUP_TILES):
             quantise(last, s, 1)

@@ -217,16 +217,14 @@ def tile_minerva_old_pa_t_kernel(tc, features, ex_features, g_weight, out_0, out
                 store(c, 0, TILES)
 
         w_sb = keep.tile([P, F_TILES * K], BF16)
-        load(0, 0, 1)
-        load(0, 1, 1)
-        nc.sync.dma_start(
-            out=w_sb[:].rearrange("p (j k) -> p j k", j=F_TILES),
-            in_=g_weight.rearrange("(j p) k -> p j k", p=P),
-        )
-        load(0, 2, 1)
-        load(0, 3, 1)
-        for half in range(GROUPS):
-            load(1, half * GROUP_TILES, GROUP_TILES)
+        for j in range(F_TILES):
+            nc.sync.dma_start(
+                out=w_sb[:, j * K : (j + 1) * K], in_=g_weight[j * P : (j + 1) * P, :]
+            )
+        for t in range(TILES):
+            load(0, t, 1)
+        for t in range(TILES):
+            load(1, t, 1)
         for c in range(2, LOADS_AHEAD):
             load(c, 0, TILES)
 
@@ -246,23 +244,21 @@ def tile_minerva_old_pa_t_kernel(tc, features, ex_features, g_weight, out_0, out
             c, half = divmod(i, GROUPS)
             if half == 0 and c + LOADS_AHEAD < n_chunks:
                 load(c + LOADS_AHEAD, 0, TILES)
+            if i == 0:
+                transpose_weight()
             transpose(i)
             if i >= 1:
                 quantise(i - 1)
-            if half == 0 and 1 <= i < n_groups - GROUPS:
+            if half == 0 and GROUPS < i < n_groups - GROUPS:
                 follow(i - 1)
                 sort(i + GROUPS, GROUP_TILES - 1)
-            if i == 3:
-                multiply(0)
-            if i >= 3:
+            if i >= 2:
                 multiply(i - 2)
             if i >= 3:
                 square_and_sum(i - 3)
             regroup_tile(nc.scalar.copy, i, 0)
             regroup_tile(nc.vector.tensor_copy if half == 0 else nc.scalar.copy, i, 1)
             if i == 0:
-                transpose_weight()
-            if i == 1:
                 quantise_weight()
             if i >= 4:
                 scale(i - 4)
@@ -270,6 +266,7 @@ def tile_minerva_old_pa_t_kernel(tc, features, ex_features, g_weight, out_0, out
             if i >= 3:
                 inverse_norms(i - 3)
 
+        ends = [(h, s) for h in (last - 1, last) for s in range(GROUP_TILES)]
         for s in range(GROUP_TILES):
             quantise(last, s, 1)
         multiply(last - 1)
@@ -278,17 +275,16 @@ def tile_minerva_old_pa_t_kernel(tc, features, ex_features, g_weight, out_0, out
         scale(last - 3)
         store_group(last - 3)
         square_and_sum(last - 2)
-        square_and_sum(last - 1)
+        square_and_sum(*ends[0], 1)
         inverse_norms(last - 2)
         scale(last - 2)
         store_group(last - 2)
-        inverse_norms(last - 1)
-        scale(last - 1)
-        store_group(last - 1)
-        for s in range(GROUP_TILES):
-            square_and_sum(last, s, 1)
-        for s in range(GROUP_TILES):
-            inverse_norms(last, s, 1)
-        for s in range(GROUP_TILES):
-            scale(last, s, 1)
-            store(n_chunks - 1, GROUP_TILES + s, 1)
+        for n, (h, s) in enumerate(ends):
+            if n + 1 < len(ends):
+                square_and_sum(*ends[n + 1], 1)
+            inverse_norms(h, s, 1)
+            scale(h, s, 1)
+            if h == last:
+                store(n_chunks - 1, GROUP_TILES + s, 1)
+            elif s == GROUP_TILES - 1:
+                store_group(h)

@@ -19,14 +19,13 @@ BLOCKS = PASSES * PAIRS
 ROW_WORDS = K // 2
 F_OUT = 256
 F_TILES = F_OUT // P
-TILES = 4
+TILES = 8
 CHUNK_ROWS = P * TILES
 GROUP_TILES = 2
 GROUPS = TILES // GROUP_TILES
 TILE_CODES = PASSES * P
 GROUP_CODES = GROUP_TILES * TILE_CODES
-FINE_CHUNKS = 3
-LOADS_AHEAD = 7
+HALVED_CHUNKS = 2
 EPS = 1e-12
 
 FLOPS = 2 * (2048 + 6144) * K * F_OUT
@@ -66,12 +65,12 @@ def tile_minerva_old_pa_t_kernel(tc, features, ex_features, g_weight, out_0, out
     n_groups = n_chunks * GROUPS
 
     with tc.manual_schedule(), tc.tile_pool(name="keep", bufs=1) as keep, tc.tile_pool(
-        name="x", bufs=LOADS_AHEAD + 1
+        name="x", bufs=n_chunks
     ) as x_pool, tc.tile_pool(name="ordered", bufs=2) as ordered_pool, tc.tile_pool(
         name="operand", bufs=4
     ) as operand_pool, tc.tile_pool(
         name="small", bufs=4
-    ) as small_pool, tc.tile_pool(name="result", bufs=6) as result_pool, tc.psum_pool(
+    ) as small_pool, tc.tile_pool(name="result", bufs=5) as result_pool, tc.psum_pool(
         name="flip", bufs=2 * GROUP_TILES
     ) as flip_pool, tc.psum_pool(name="product", bufs=4) as product_pool:
         x_tiles = {}
@@ -109,8 +108,8 @@ def tile_minerva_old_pa_t_kernel(tc, features, ex_features, g_weight, out_0, out
             )
 
         def tile_words(h, s):
-            c, half = divmod(h, GROUPS)
-            first = (half * GROUP_TILES + s) * ROW_WORDS
+            c, part = divmod(h, GROUPS)
+            first = (part * GROUP_TILES + s) * ROW_WORDS
             return x_tiles[c][:].bitcast(F32)[:, first : first + ROW_WORDS]
 
         def sort(h, s):
@@ -187,11 +186,11 @@ def tile_minerva_old_pa_t_kernel(tc, features, ex_features, g_weight, out_0, out
             inverses[h, first_tile] = inverse
 
         def scale(h, first_tile=0, tiles=GROUP_TILES):
-            c, half = divmod(h, GROUPS)
-            if half == 0 and first_tile == 0:
+            c, part = divmod(h, GROUPS)
+            if part == 0 and first_tile == 0:
                 result = result_pool.tile([P, TILES, F_OUT], F32)
                 results[c] = result
-            t = half * GROUP_TILES + first_tile
+            t = part * GROUP_TILES + first_tile
             nc.vector.scalar_tensor_tensor(
                 out=results[c][:, t : t + tiles, :],
                 in0=inverses[h, first_tile][:].unsqueeze(2).to_broadcast([P, tiles, F_OUT]),
@@ -210,23 +209,25 @@ def tile_minerva_old_pa_t_kernel(tc, features, ex_features, g_weight, out_0, out
             )
 
         def store_group(h):
-            c, half = divmod(h, GROUPS)
-            if c >= n_chunks - FINE_CHUNKS:
-                store(c, half * GROUP_TILES, GROUP_TILES)
-            elif half == GROUPS - 1:
-                store(c, 0, TILES)
+            c, part = divmod(h, GROUPS)
+            pieces = {n_chunks - 1: GROUPS, n_chunks - 2: 2}.get(c, 1)
+            groups = GROUPS // pieces
+            if part % groups == groups - 1:
+                store(c, (part + 1 - groups) * GROUP_TILES, groups * GROUP_TILES)
 
         w_sb = keep.tile([P, F_TILES * K], BF16)
         for j in range(F_TILES):
             nc.sync.dma_start(
                 out=w_sb[:, j * K : (j + 1) * K], in_=g_weight[j * P : (j + 1) * P, :]
             )
-        for t in range(TILES):
-            load(0, t, 1)
-        for t in range(TILES):
-            load(1, t, 1)
-        for c in range(2, LOADS_AHEAD):
-            load(c, 0, TILES)
+        load(0, 0, 1)
+        load(0, 1, 1)
+        for first_tile in range(GROUP_TILES, TILES, GROUP_TILES):
+            load(0, first_tile, GROUP_TILES)
+        for c in range(1, n_chunks):
+            pieces = 2 if c <= HALVED_CHUNKS else 1
+            for piece in range(pieces):
+                load(c, piece * TILES // pieces, TILES // pieces)
 
         w_grouped = keep.tile([P, PASSES * F_OUT * PACK], BF16, align_bytes=64)
         w_codes = keep.tile([P, PASSES * F_OUT], U32, align_bytes=64)
@@ -241,23 +242,21 @@ def tile_minerva_old_pa_t_kernel(tc, features, ex_features, g_weight, out_0, out
 
         last = n_groups - 1
         for i in range(n_groups):
-            c, half = divmod(i, GROUPS)
-            if half == 0 and c + LOADS_AHEAD < n_chunks:
-                load(c + LOADS_AHEAD, 0, TILES)
+            even = i % 2 == 0
             if i == 0:
                 transpose_weight()
             transpose(i)
             if i >= 1:
                 quantise(i - 1)
-            if half == 0 and GROUPS < i < n_groups - GROUPS:
+            if even and 2 < i < n_groups - 2:
                 follow(i - 1)
-                sort(i + GROUPS, GROUP_TILES - 1)
+                sort(i + 2, GROUP_TILES - 1)
             if i >= 2:
                 multiply(i - 2)
             if i >= 3:
                 square_and_sum(i - 3)
             regroup_tile(nc.scalar.copy, i, 0)
-            regroup_tile(nc.vector.tensor_copy if half == 0 else nc.scalar.copy, i, 1)
+            regroup_tile(nc.vector.tensor_copy if even else nc.scalar.copy, i, 1)
             if i == 0:
                 quantise_weight()
             if i >= 4:
@@ -285,6 +284,6 @@ def tile_minerva_old_pa_t_kernel(tc, features, ex_features, g_weight, out_0, out
             inverse_norms(h, s, 1)
             scale(h, s, 1)
             if h == last:
-                store(n_chunks - 1, GROUP_TILES + s, 1)
+                store(n_chunks - 1, TILES - GROUP_TILES + s, 1)
             elif s == GROUP_TILES - 1:
                 store_group(h)

import concourse.mybir as mybir
from concourse.masks import make_identity

F32 = mybir.dt.float32
BF16 = mybir.dt.bfloat16
U32 = mybir.dt.uint32
U8 = mybir.dt.uint8
FP8X4 = mybir.dt.float8_e4m3fn_x4
ACT = mybir.ActivationFunctionType
ALU = mybir.AluOpType

P = 128
PACK = 4
K = 1024
K_PASS = P * PACK
PASSES = K // K_PASS
PAIRS = PACK // 2
BLOCKS = PASSES * PAIRS
ROW_WORDS = K // 2
F_OUT = 256
F_TILES = F_OUT // P
TILES = 8
CHUNK_ROWS = P * TILES
GROUP_TILES = 2
GROUPS = TILES // GROUP_TILES
TILE_CODES = PASSES * P
GROUP_CODES = GROUP_TILES * TILE_CODES
HALVED_CHUNKS = 2
EPS = 1e-12

FLOPS = 2 * (2048 + 6144) * K * F_OUT


def transpose_rows(nc, flip_pool, identity, rows_words, in_order=False):
    flipped = flip_pool.tile([P, BLOCKS, P], F32)
    for b in range(BLOCKS):
        g, u = divmod(b, PAIRS)
        if in_order:
            block_words = slice(b * P, (b + 1) * P)
        else:
            block_words = slice(g * PAIRS * P + u, (g + 1) * PAIRS * P, PAIRS)
        nc.tensor.transpose(flipped[:, b, :], rows_words[:, block_words], identity[:])
    return flipped


def sort_words(copy, ordered_words, rows_words):
    copy(
        out=ordered_words.rearrange("r (g u j) -> r g u j", g=PASSES, u=PAIRS),
        in_=rows_words.rearrange("r (g j u) -> r g u j", g=PASSES, u=PAIRS),
    )


def regroup(copy, flipped, grouped_words):
    copy(out=grouped_words, in_=flipped[:].rearrange("p (g u) r -> p g r u", u=PAIRS))


def tile_minerva_old_pa_t_kernel(tc, features, ex_features, g_weight, out_0, out_1):
    nc = tc.nc

    chunks = []
    for src, dst in ((features, out_0), (ex_features, out_1)):
        for row in range(0, src.shape[0], CHUNK_ROWS):
            chunks.append((src[row : row + CHUNK_ROWS, :], dst[row : row + CHUNK_ROWS, :]))
    n_chunks = len(chunks)
    n_groups = n_chunks * GROUPS

    with tc.manual_schedule(), tc.tile_pool(name="keep", bufs=1) as keep, tc.tile_pool(
        name="x", bufs=n_chunks
    ) as x_pool, tc.tile_pool(name="ordered", bufs=2) as ordered_pool, tc.tile_pool(
        name="operand", bufs=4
    ) as operand_pool, tc.tile_pool(
        name="small", bufs=4
    ) as small_pool, tc.tile_pool(name="result", bufs=5) as result_pool, tc.psum_pool(
        name="flip", bufs=2 * GROUP_TILES
    ) as flip_pool, tc.psum_pool(name="product", bufs=4) as product_pool:
        x_tiles = {}
        ordered_tiles = {}
        flipped_tiles = {}
        operands = {}
        products = {}
        sums = {}
        inverses = {}
        results = {}

        def load(c, first_tile, tiles):
            if first_tile == 0:
                x_sb = x_pool.tile([P, TILES * K], BF16)
                x_tiles[c] = x_sb
            rows = chunks[c][0].rearrange("(p t) k -> p (t k)", t=TILES)
            cols = slice(first_tile * K, (first_tile + tiles) * K)
            nc.sync.dma_start(out=x_tiles[c][:, cols], in_=rows[:, cols])

        def transpose_weight():
            w_words = w_sb[:].bitcast(F32)
            w_grouped_words = w_grouped[:].bitcast(F32).rearrange(
                "p (g j r u) -> p j g r u", g=PASSES, j=F_TILES, u=PAIRS
            )
            w_copies = (nc.vector.tensor_copy, nc.scalar.copy)
            for j in range(F_TILES):
                w_flipped = transpose_rows(
                    nc, flip_pool, identity, w_words[:, j * ROW_WORDS : (j + 1) * ROW_WORDS]
                )
                regroup(w_copies[j], w_flipped, w_grouped_words[:, j])

        def quantise_weight():
            nc.vector.quantize_mx(
                out=w_codes[:].bitcast(FP8X4), scales=w_scales[:], in_=w_grouped[:]
            )

        def tile_words(h, s):
            c, part = divmod(h, GROUPS)
            first = (part * GROUP_TILES + s) * ROW_WORDS
            return x_tiles[c][:].bitcast(F32)[:, first : first + ROW_WORDS]

        def sort(h, s):
            ordered = ordered_pool.tile([P, ROW_WORDS], F32)
            sort_words(nc.gpsimd.tensor_copy, ordered[:], tile_words(h, s))
            ordered_tiles[h, s] = ordered

        def follow(h):
            word = ordered_pool.tile([P, 1], U32)
            nc.gpsimd.tensor_copy(out=word[:], in_=operands[h][1][:, 0:1])

        def transpose(h):
            flipped_tiles[h] = []
            for s in range(GROUP_TILES):
                in_order = (h, s) in ordered_tiles
                words = ordered_tiles[h, s][:] if in_order else tile_words(h, s)
                flipped_tiles[h].append(transpose_rows(nc, flip_pool, identity, words, in_order))
            grouped = operand_pool.tile([P, GROUP_CODES * PACK], BF16, align_bytes=64)
            codes = operand_pool.tile([P, GROUP_CODES], U32, align_bytes=64)
            scales = operand_pool.tile([P, GROUP_CODES], U8, align_bytes=64)
            operands[h] = (grouped, codes, scales)

        def regroup_tile(copy, h, s):
            grouped_words = operands[h][0][:].bitcast(F32).rearrange(
                "p (s g r u) -> p s g r u", s=GROUP_TILES, g=PASSES, u=PAIRS
            )
            regroup(copy, flipped_tiles[h][s], grouped_words[:, s])

        def quantise(h, first_tile=0, tiles=GROUP_TILES):
            grouped, codes, scales = operands[h]
            cols = slice(first_tile * TILE_CODES, (first_tile + tiles) * TILE_CODES)
            values = slice(cols.start * PACK, cols.stop * PACK)
            nc.vector.quantize_mx(
                out=codes[:, cols].bitcast(FP8X4), scales=scales[:, cols], in_=grouped[:, values]
            )

        def multiply(h, first_tile=0, tiles=GROUP_TILES):
            grouped, codes, scales = operands[h]
            if first_tile == 0:
                product = product_pool.tile([P, GROUP_TILES, F_OUT], F32)
                products[h] = product
            for s in range(first_tile, first_tile + tiles):
                for g in range(PASSES):
                    first = (s * PASSES + g) * P
                    row_cols = slice(first, first + P)
                    outs = slice(g * F_OUT, (g + 1) * F_OUT)
                    nc.tensor.matmul_mx(
                        out=products[h][:, s, :],
                        lhsT=codes[:, row_cols].bitcast(FP8X4),
                        lhsT_scale=scales[:, row_cols],
                        rhs=w_codes[:, outs].bitcast(FP8X4),
                        rhs_scale=w_scales[:, outs],
                        start=(g == 0),
                        stop=(g == PASSES - 1),
                    )

        def square_and_sum(h, first_tile=0, tiles=GROUP_TILES):
            sum_sq = small_pool.tile([P, tiles], F32)
            for s in range(tiles):
                unread = small_pool.tile([P, F_OUT], F32)
                nc.scalar.activation(
                    out=unread[:],
                    in_=products[h][:, first_tile + s, :],
                    func=ACT.Square,
                    accum_out=sum_sq[:, s : s + 1],
                )
            sums[h, first_tile] = sum_sq

        def inverse_norms(h, first_tile=0, tiles=GROUP_TILES):
            inverse = small_pool.tile([P, tiles], F32)
            nc.scalar.activation(
                out=inverse[:], in_=sums[h, first_tile][:], func=ACT.Abs_reciprocal_sqrt
            )
            inverses[h, first_tile] = inverse

        def scale(h, first_tile=0, tiles=GROUP_TILES):
            c, part = divmod(h, GROUPS)
            if part == 0 and first_tile == 0:
                result = result_pool.tile([P, TILES, F_OUT], F32)
                results[c] = result
            t = part * GROUP_TILES + first_tile
            nc.vector.scalar_tensor_tensor(
                out=results[c][:, t : t + tiles, :],
                in0=inverses[h, first_tile][:].unsqueeze(2).to_broadcast([P, tiles, F_OUT]),
                scalar=1.0 / EPS,
                in1=products[h][:, first_tile : first_tile + tiles, :],
                op0=ALU.min,
                op1=ALU.mult,
            )

        def store(c, first_tile, tiles):
            nc.sync.dma_start(
                out=chunks[c][1].rearrange("(p t) f -> p t f", t=TILES)[
                    :, first_tile : first_tile + tiles, :
                ],
                in_=results[c][:, first_tile : first_tile + tiles, :],
            )

        def store_group(h):
            c, part = divmod(h, GROUPS)
            pieces = {n_chunks - 1: GROUPS, n_chunks - 2: 2}.get(c, 1)
            groups = GROUPS // pieces
            if part % groups == groups - 1:
                store(c, (part + 1 - groups) * GROUP_TILES, groups * GROUP_TILES)

        w_sb = keep.tile([P, F_TILES * K], BF16)
        for j in range(F_TILES):
            nc.sync.dma_start(
                out=w_sb[:, j * K : (j + 1) * K], in_=g_weight[j * P : (j + 1) * P, :]
            )
        load(0, 0, 1)
        load(0, 1, 1)
        for first_tile in range(GROUP_TILES, TILES, GROUP_TILES):
            load(0, first_tile, GROUP_TILES)
        for c in range(1, n_chunks):
            pieces = 2 if c <= HALVED_CHUNKS else 1
            for piece in range(pieces):
                load(c, piece * TILES // pieces, TILES // pieces)

        w_grouped = keep.tile([P, PASSES * F_OUT * PACK], BF16, align_bytes=64)
        w_codes = keep.tile([P, PASSES * F_OUT], U32, align_bytes=64)
        w_scales = keep.tile([P, PASSES * F_OUT], U8, align_bytes=64)
        identity = keep.tile([P, P], F32)
        make_identity(nc, identity[:])

        one = keep.tile([P, 1], F32)
        nc.vector.memset(one[:], 1.0)
        warm = keep.tile([P, 1], F32)
        nc.scalar.activation(out=warm[:], in_=one[:], func=ACT.Abs_reciprocal_sqrt)

        last = n_groups - 1
        for i in range(n_groups):
            even = i % 2 == 0
            if i == 0:
                transpose_weight()
            transpose(i)
            if i >= 1:
                quantise(i - 1)
            if even and 2 < i < n_groups - 2:
                follow(i - 1)
                sort(i + 2, GROUP_TILES - 1)
            if i >= 2:
                multiply(i - 2)
            if i >= 3:
                square_and_sum(i - 3)
            regroup_tile(nc.scalar.copy, i, 0)
            regroup_tile(nc.vector.tensor_copy if even else nc.scalar.copy, i, 1)
            if i == 0:
                quantise_weight()
            if i >= 4:
                scale(i - 4)
                store_group(i - 4)
            if i >= 3:
                inverse_norms(i - 3)

        ends = [(h, s) for h in (last - 1, last) for s in range(GROUP_TILES)]
        for s in range(GROUP_TILES):
            quantise(last, s, 1)
        multiply(last - 1)
        for s in range(GROUP_TILES):
            multiply(last, s, 1)
        scale(last - 3)
        store_group(last - 3)
        square_and_sum(last - 2)
        square_and_sum(*ends[0], 1)
        inverse_norms(last - 2)
        scale(last - 2)
        store_group(last - 2)
        for n, (h, s) in enumerate(ends):
            if n + 1 < len(ends):
                square_and_sum(*ends[n + 1], 1)
            inverse_norms(h, s, 1)
            scale(h, s, 1)
            if h == last:
                store(n_chunks - 1, TILES - GROUP_TILES + s, 1)
            elif s == GROUP_TILES - 1:
                store_group(h)
